import numpy as np
import ml_dtypes


def mxq(x, axis, fmt="e4m3"):
    dtype, down = {"e4m3": (ml_dtypes.float8_e4m3fn, 7), "e5m2": (ml_dtypes.float8_e5m2, 14)}[fmt]
    v = np.moveaxis(np.asarray(x, np.float32).astype(ml_dtypes.bfloat16).astype(np.float64), axis, -1)
    blocks = v.reshape(v.shape[:-1] + (-1, 32))
    amax = np.abs(blocks).max(-1, keepdims=True)
    byte = np.maximum(np.where(amax > 0, np.frexp(amax)[1] - 1 + 127, 0) - down, 1)
    scale = np.exp2(byte - 127.0)
    codes = (blocks / scale).astype(np.float32).astype(dtype).astype(np.float64)
    return np.moveaxis((codes * scale).reshape(v.shape), -1, axis)


WIDE = False


def mx_kscale(k):
    if not WIDE:
        return np.ones(k)
    levels = np.array([10, -10, 5, -5, 0])
    a = np.random.permutation(np.resize(levels, k // 512 * 4)).reshape(k // 512, 4)
    idx = np.arange(k)
    return np.exp2(a[idx // 512, idx % 128 // 32])


BF16 = ml_dtypes.bfloat16


def bf(x):
    return np.asarray(x, np.float32).astype(BF16)


def f64(x):
    return np.asarray(x).astype(np.float64)


E2M1 = np.array([0.0, 0.5, 1.0, 1.5, 2.0, 3.0, 4.0, 6.0, -0.0, -0.5, -1.0, -1.5, -2.0, -3.0, -4.0, -6.0])


def pack_weight(w, fmt):
    k, n = w.shape
    w = f64(bf(w)).reshape(k // 32, 32, n)
    amax = np.abs(w).max(1)
    if fmt == "e4m3":
        byte = np.frexp(amax)[1] - 1 + 127 - 7
    else:
        mant, ex = np.frexp(amax / 6.0)
        byte = np.where(mant > 0.5, ex, ex - 1) + 127
    byte = np.clip(np.where(amax > 0, byte, 1), 1, 254)
    scaled = (w * np.exp2(127.0 - byte)[:, None, :]).reshape(k, n).astype(np.float32)
    by_word = np.ascontiguousarray(scaled.reshape(k // 512, 128, 4, n).transpose(0, 1, 3, 2))
    if fmt == "e4m3":
        words = by_word.astype(ml_dtypes.float8_e4m3fn).view(np.uint8)
    else:
        c = by_word.astype(ml_dtypes.float4_e2m1fn).view(np.uint8) & 0xF
        words = c[..., 0::2] | (c[..., 1::2] << 4)
    return np.ascontiguousarray(words), np.ascontiguousarray(byte.astype(np.uint8).reshape(k // 512, 16, n))


def unpack_weight(words, scales, fmt):
    g, p, n, _ = words.shape
    if fmt == "e4m3":
        vals = np.ascontiguousarray(words).view(ml_dtypes.float8_e4m3fn).astype(np.float64)
    else:
        nib = np.empty((g, p, n, 4), np.uint8)
        nib[..., 0::2] = words & 0xF
        nib[..., 1::2] = words >> 4
        vals = E2M1[nib]
    vals = vals * np.repeat(np.exp2(scales.astype(np.float64) - 127.0), 8, axis=1)[..., None]
    return vals.transpose(0, 1, 3, 2).reshape(g * 512, n)


B, T, U, D_ENC, D_PRED, D_JOINT, VOCAB = 64, 2, 2, 2048, 2048, 4096, 2048
LOGIT_CLAMP = 15.0
FMT = "e4m3"


def setup_inputs():
    se, sp = mx_kscale(D_ENC), mx_kscale(D_PRED)
    t = mx_kscale(D_JOINT)
    g = t / t.max()
    encoder_out = bf(np.random.standard_normal((B, T, D_ENC)) * se)
    predictor_out = bf(np.random.standard_normal((B, U, D_PRED)) * sp)
    W_enc_words, W_enc_scales = pack_weight(np.random.standard_normal((D_ENC, D_JOINT)) * 0.7 / np.sqrt(D_ENC) / se[:, None] * g, FMT)
    b_enc = bf(np.random.standard_normal(D_JOINT) * 0.2 * g)
    W_pred_words, W_pred_scales = pack_weight(np.random.standard_normal((D_PRED, D_JOINT)) * 0.7 / np.sqrt(D_PRED) / sp[:, None] * g, FMT)
    b_pred = bf(np.random.standard_normal(D_JOINT) * 0.2 * g)
    W_out_words, W_out_scales = pack_weight(np.random.standard_normal((D_JOINT, VOCAB)) * 8.0 / np.sqrt(D_JOINT) / g[:, None], FMT)
    b_out = bf(np.random.standard_normal(VOCAB) * 0.5)
    return {"encoder_out": encoder_out,
            "predictor_out": predictor_out,
            "W_enc_words": W_enc_words,
            "W_enc_scales": W_enc_scales,
            "b_enc": b_enc,
            "W_pred_words": W_pred_words,
            "W_pred_scales": W_pred_scales,
            "b_pred": b_pred,
            "W_out_words": W_out_words,
            "W_out_scales": W_out_scales,
            "b_out": b_out}


def reference(encoder_out, predictor_out, W_enc_words, W_enc_scales, b_enc, W_pred_words, W_pred_scales, b_pred, W_out_words, W_out_scales, b_out):
    enc = (mxq(f64(encoder_out), 2, "e4m3") @ unpack_weight(W_enc_words, W_enc_scales, FMT)) + f64(b_enc)
    pred = (mxq(f64(predictor_out), 2, "e4m3") @ unpack_weight(W_pred_words, W_pred_scales, FMT)) + f64(b_pred)
    joint = np.tanh(enc[:, :, None, :] + pred[:, None, :, :])
    logits = (mxq(joint, 3, "e4m3") @ unpack_weight(W_out_words, W_out_scales, FMT)) + f64(b_out)
    return np.clip(logits, -LOGIT_CLAMP, LOGIT_CLAMP)

@@ -1,0 +1,265 @@
+from contextlib import ExitStack
+
+import concourse.mybir as mybir
+from concourse.masks import make_identity
+
+F32 = mybir.dt.float32
+BF16 = mybir.dt.bfloat16
+I32 = mybir.dt.int32
+U32 = mybir.dt.uint32
+U8 = mybir.dt.uint8
+FP8X4 = mybir.dt.float8_e4m3fn_x4
+ADD = mybir.AluOpType.add
+MIN = mybir.AluOpType.min
+MAX = mybir.AluOpType.max
+TANH = mybir.ActivationFunctionType.Tanh
+
+P = 128
+FLOPS = 2 * 128 * 2048 * 4096 * 2 + 2 * 256 * 4096 * 2048
+CLAMP = 15.0
+
+
+def tile_jointnetwork_w_kernel(
+    tc,
+    encoder_out,
+    predictor_out,
+    W_enc_words,
+    W_enc_scales,
+    b_enc,
+    W_pred_words,
+    W_pred_scales,
+    b_pred,
+    W_out_words,
+    W_out_scales,
+    b_out,
+    out,
+):
+    nc = tc.nc
+    with ExitStack() as ctx:
+        const = ctx.enter_context(tc.tile_pool(name="const", bufs=1))
+        wpool = ctx.enter_context(tc.tile_pool(name="wpool", bufs=16))
+        work = ctx.enter_context(tc.tile_pool(name="work", bufs=2))
+        psum = ctx.enter_context(tc.psum_pool(name="psum", bufs=1))
+
+        def bank(k, shape, name):
+            return psum.tile(shape, F32, tag="b%d" % k, name=name)
+
+        pl_enc = const.tile([P, 4096], U8, align_bytes=64)
+        pl_pred = const.tile([P, 4096], U8, align_bytes=64)
+        pl_out = const.tile([P, 2, 2048], U8, align_bytes=64)
+        nc.vector.memset(pl_enc[:].bitcast(I32), 0)
+        nc.vector.memset(pl_pred[:].bitcast(I32), 0)
+        nc.vector.memset(pl_out[:].bitcast(I32), 0)
+        warm = const.tile([P, 1], F32)
+        nc.vector.memset(warm[:], 0.0)
+        nc.scalar.activation(out=warm[:], in_=warm[:], func=TANH)
+
+        ident = const.tile([P, P], F32)
+        make_identity(nc, ident[:])
+        brow = const.tile([P, 512], BF16)
+        nc.gpsimd.memset(brow[:].bitcast(F32), 0.0)
+        borow = const.tile([P, 2048], BF16)
+        nc.gpsimd.memset(borow[:].bitcast(F32), 0.0)
+        ones = const.tile([P, P], BF16)
+        nc.gpsimd.memset(ones[:], 1.0)
+
+        xe = const.tile([P, 2048], BF16)
+        xp = const.tile([P, 2048], BF16)
+        nc.sync.dma_start(out=xe[:], in_=encoder_out.flatten_outer_dims())
+        nc.sync.dma_start(out=xp[:], in_=predictor_out.flatten_outer_dims())
+        nc.scalar.dma_start(out=brow[0:8, :], in_=b_enc.rearrange("(g c) -> g c", g=8))
+        nc.scalar.dma_start(out=brow[8:16, :], in_=b_pred.rearrange("(g c) -> g c", g=8))
+        nc.scalar.dma_start(out=borow[0:1, :], in_=b_out.rearrange("(o n) -> o n", o=1))
+
+        for sc, pl in ((W_enc_scales, pl_enc), (W_pred_scales, pl_pred)):
+            sc32 = sc.bitcast(I32)
+            pl32 = pl[:].bitcast(I32)
+            for q in (0, 2, 1, 3):
+                nc.sync.dma_start(out=pl32[32 * q : 32 * q + 16, :], in_=sc32[:, 4 * q : 4 * q + 4, :])
+
+        we32 = W_enc_words.bitcast(I32).rearrange("g p n o -> p g (n o)")
+        wp32 = W_pred_words.bitcast(I32).rearrange("g p n o -> p g (n o)")
+        wo32 = W_out_words.bitcast(I32).rearrange("g p n o -> p g (n o)")
+
+        s1w = []
+        for qt in range(4):
+            both = []
+            for nm, w32 in (("e", we32), ("p", wp32)):
+                halves = []
+                for gp in range(2):
+                    t = wpool.tile([P, 2, 1024], I32, tag="w", name="w%s%d%d" % (nm, qt, gp), align_bytes=64)
+                    nc.sync.dma_start(out=t[:], in_=w32[:, 2 * gp : 2 * gp + 2, 1024 * qt : 1024 * (qt + 1)])
+                    halves.append(t)
+                both.append(halves)
+            s1w.append(both)
+
+        so32 = W_out_scales.bitcast(I32)
+        po32 = pl_out[:].bitcast(I32)
+        for a in range(2):
+            for q in (0, 2, 1, 3):
+                nc.sync.dma_start(
+                    out=po32[32 * q : 32 * q + 16, a, :],
+                    in_=so32[4 * a : 4 * a + 4, 4 * q : 4 * q + 4, :],
+                )
+
+        xq = []
+        xs = []
+        for n, (x_sb, nm) in enumerate(((xe, "e"), (xp, "p"))):
+            xw = x_sb[:].bitcast(F32)
+            grp = const.tile([P, 4, P, 4], BF16, name="grp" + nm, align_bytes=64)
+            grp32 = grp[:].rearrange("p g r t -> p g (r t)").bitcast(F32).rearrange("p g (r u) -> p g r u", u=2)
+            for gp in range(2):
+                xt = bank(2 * n + gp, [P, 2, 2, P], "xt%s%d" % (nm, gp))
+                for gg in range(2):
+                    g = 2 * gp + gg
+                    for u in range(2):
+                        nc.tensor.transpose(xt[:, gg, u, :], xw[:, 256 * g + u : 256 * (g + 1) : 2], ident[:])
+                src = xt[:].rearrange("p g u r -> p g r u")
+                if n == 0:
+                    nc.vector.tensor_copy(out=grp32[:, 2 * gp : 2 * gp + 2, :, :], in_=src)
+                else:
+                    nc.scalar.copy(out=grp32[:, 2 * gp : 2 * gp + 2, :, :], in_=src)
+            q_t = const.tile([P, 512], U32, name="xq" + nm, align_bytes=64)
+            s_t = const.tile([P, 512], U8, name="xs" + nm, align_bytes=64)
+            nc.vector.quantize_mx(
+                out=q_t[:].bitcast(FP8X4),
+                scales=s_t[:],
+                in_=grp[:].rearrange("p g r t -> p (g r t)"),
+            )
+            xq.append(q_t)
+            xs.append(s_t)
+
+        bias_out = const.tile([P, 2048], F32)
+        for c in range(4):
+            bo = bank(4 + c, [P, 512], "bo%d" % c)
+            nc.tensor.matmul(out=bo[:], lhsT=ones[:], rhs=borow[:, 512 * c : 512 * (c + 1)], start=True, stop=True)
+            if c % 2 == 0:
+                nc.vector.tensor_copy(out=bias_out[:, 512 * c : 512 * (c + 1)], in_=bo[:])
+            else:
+                nc.scalar.copy(out=bias_out[:, 512 * c : 512 * (c + 1)], in_=bo[:])
+        bt = bank(4, [P, 2, P], "bt")
+        bw = brow[:].bitcast(F32)
+        for u in range(2):
+            nc.tensor.transpose(bt[:, u, :], bw[:, u : 256 : 2], ident[:])
+        bc = const.tile([P, 16, 2, 2], F32)
+        btv = bt[:].bitcast(BF16).rearrange("p u (r e) -> p u r e", e=2)
+        nc.vector.tensor_copy(out=bc[:], in_=btv[:, :, 0:16, :].rearrange("p u r e -> p r u e"))
+        bias_j = const.tile([P, 8, 4], F32)
+        bcv = bc[:].rearrange("p r u e -> p r (u e)")
+        nc.vector.tensor_tensor(out=bias_j[:], in0=bcv[:, 0:8, :], in1=bcv[:, 8:16, :], op=ADD)
+
+        jq = const.tile([P, 8, 256], U32, align_bytes=64)
+        jp = const.tile([P, 8, 256], U8, align_bytes=64)
+        planes = (pl_enc, pl_pred)
+        wout = []
+
+        def stage1_sums(qt, n):
+            sums = [bank(2 * n + jj, [P, 512], "s1_%d_%d_%d" % (n, qt, jj)) for jj in range(2)]
+            for g in range(4):
+                for jj in range(2):
+                    nc.tensor.matmul_mx(
+                        out=sums[jj][:],
+                        lhsT=xq[n][:, P * g : P * (g + 1)].bitcast(FP8X4),
+                        lhsT_scale=xs[n][:, P * g : P * (g + 1)],
+                        rhs=s1w[qt][n][g // 2][:, g % 2, 512 * jj : 512 * (jj + 1)].bitcast(FP8X4),
+                        rhs_scale=planes[n][4 * g : P, 1024 * qt + 512 * jj : 1024 * qt + 512 * (jj + 1)],
+                        start=(g == 0),
+                        stop=(g == 3),
+                    )
+            sorted_tiles = []
+            for jj in range(2):
+                srt = work.tile([P, 4, P], F32, tag="srt%d" % n, name="srt%d_%d_%d" % (n, qt, jj))
+                nc.scalar.copy(out=srt[:], in_=sums[jj][:].rearrange("r (p t) -> r t p", t=4))
+                sorted_tiles.append(srt)
+            flipped = []
+            for jj in range(2):
+                fl = bank(4 + 2 * n + jj, [P, 4, P], "fl%d_%d_%d" % (n, qt, jj))
+                for t4 in range(4):
+                    nc.tensor.transpose(fl[:, t4, :], sorted_tiles[jj][:, t4, :], ident[:])
+                flipped.append(fl)
+            return flipped
+
+        for qt in range(4):
+            enc_t = stage1_sums(qt, 0)
+            e1s = []
+            for jj in range(2):
+                e1 = work.tile([P, P, 4], F32, tag="e1", name="e1_%d_%d" % (qt, jj))
+                nc.vector.tensor_tensor(
+                    out=e1[:],
+                    in0=enc_t[jj][:].rearrange("p t r -> p r t"),
+                    in1=bias_j[:, 2 * qt + jj, :].unsqueeze(1).to_broadcast([P, P, 4]),
+                    op=ADD,
+                )
+                e1s.append(e1)
+            pred_t = stage1_sums(qt, 1)
+            if qt < 2:
+                for c in range(4 * qt, 4 * qt + 4):
+                    h, gp = c // 4, c % 4
+                    t = wpool.tile([P, 2, 1024], I32, tag="w", name="wo%d" % c, align_bytes=64)
+                    cols = slice(1024 * h, 1024 * (h + 1))
+                    if c < 7:
+                        nc.sync.dma_start(out=t[:], in_=wo32[:, 2 * gp : 2 * gp + 2, cols])
+                    else:
+                        nc.sync.dma_start(out=t[:, 0, :], in_=wo32[:, 6, cols])
+                        nc.sync.dma_start(out=t[:, 1, 0:512], in_=wo32[:, 7, 1024:1536])
+                        nc.sync.dma_start(out=t[:, 1, 512:1024], in_=wo32[:, 7, 1536:2048])
+                    wout.append(t)
+            zs = []
+            for jj in range(2):
+                z = work.tile([P, 64, 2, 2, 4], F32, tag="z", name="z_%d_%d" % (qt, jj))
+                e1v = e1s[jj][:].rearrange("p (b s) t -> p b s t", s=2)
+                pv = pred_t[jj][:].rearrange("p t (b u) -> p b u t", u=2)
+                for s in range(2):
+                    nc.vector.tensor_tensor(
+                        out=z[:, :, s, :, :],
+                        in0=pv,
+                        in1=e1v[:, :, s, :].unsqueeze(2).to_broadcast([P, 64, 2, 4]),
+                        op=ADD,
+                    )
+                zs.append(z)
+            jgs = []
+            for jj in range(2):
+                jg = work.tile([P, 1024], BF16, tag="jg", name="jg_%d_%d" % (qt, jj), align_bytes=64)
+                nc.scalar.activation(out=jg[:], in_=zs[jj][:].rearrange("p b s u t -> p (b s u t)"), func=TANH)
+                jgs.append(jg)
+            for jj in range(2):
+                i = 2 * qt + jj
+                nc.vector.quantize_mx(out=jq[:, i, :].bitcast(FP8X4), scales=jp[:, i, :], in_=jgs[jj][:])
+
+        outf = out.flatten_outer_dims()
+        for h in range(2):
+            acc = [[bank(4 * h + 2 * nt + rt, [P, 512], "acc%d%d%d" % (h, nt, rt)) for rt in range(2)] for nt in range(2)]
+            for g in range(8):
+                wt = wout[4 * h + g // 2]
+                for nt in range(2):
+                    for rt in range(2):
+                        nc.tensor.matmul_mx(
+                            out=acc[nt][rt][:],
+                            lhsT=jq[:, g, P * rt : P * (rt + 1)].bitcast(FP8X4),
+                            lhsT_scale=jp[:, g, P * rt : P * (rt + 1)],
+                            rhs=wt[:, g % 2, 512 * nt : 512 * (nt + 1)].bitcast(FP8X4),
+                            rhs_scale=pl_out[4 * (g % 4) : P, g // 4, 1024 * h + 512 * nt : 1024 * h + 512 * (nt + 1)],
+                            start=(g == 0),
+                            stop=(g == 7),
+                        )
+            if h == 0:
+                for rt in range(2):
+                    st = work.tile([P, 1024], F32, tag="st", name="st%d" % rt)
+                    for nt in range(2):
+                        nc.vector.tensor_tensor(
+                            out=st[:, 512 * nt : 512 * (nt + 1)],
+                            in0=acc[nt][rt][:],
+                            in1=bias_out[:, 512 * nt : 512 * (nt + 1)],
+                            op=ADD,
+                        )
+                    nc.gpsimd.tensor_scalar(out=st[:], in0=st[:], scalar1=CLAMP, scalar2=-CLAMP, op0=MIN, op1=MAX)
+                    nc.scalar.dma_start(out=outf[P * rt : P * (rt + 1), 0:1024], in_=st[:])
+            else:
+                for nt in range(2):
+                    for rt in range(2):
+                        cols = slice(1024 + 512 * nt, 1024 + 512 * (nt + 1))
+                        sl = work.tile([P, 512], F32, tag="sl", name="sl%d%d" % (nt, rt), bufs=4)
+                        nc.vector.tensor_tensor(out=sl[:], in0=acc[nt][rt][:], in1=bias_out[:, cols], op=ADD)
+                        eng = nc.vector if (nt == 1 and rt == 1) else nc.gpsimd
+                        eng.tensor_scalar(out=sl[:], in0=sl[:], scalar1=CLAMP, scalar2=-CLAMP, op0=MIN, op1=MAX)
+                        nc.sync.dma_start(out=outf[P * rt : P * (rt + 1), cols], in_=sl[:])

@@ -253,7 +253,7 @@ def tile_jointnetwork_w_kernel(
                             op=ADD,
                         )
                     nc.gpsimd.tensor_scalar(out=st[:], in0=st[:], scalar1=CLAMP, scalar2=-CLAMP, op0=MIN, op1=MAX)
-                    nc.scalar.dma_start(out=outf[P * rt : P * (rt + 1), 0:1024], in_=st[:])
+                    nc.sync.dma_start(out=outf[P * rt : P * (rt + 1), 0:1024], in_=st[:])
             else:
                 for nt in range(2):
                     for rt in range(2):

@@ -95,12 +95,15 @@ def tile_jointnetwork_w_kernel(
 
         so32 = W_out_scales.bitcast(I32)
         po32 = pl_out[:].bitcast(I32)
-        for a in range(2):
+
+        def load_out_scales(a):
             for q in (0, 2, 1, 3):
                 nc.sync.dma_start(
                     out=po32[32 * q : 32 * q + 16, a, :],
                     in_=so32[4 * a : 4 * a + 4, 4 * q : 4 * q + 4, :],
                 )
+
+        load_out_scales(0)
 
         xq = []
         xs = []
@@ -197,8 +200,14 @@ def tile_jointnetwork_w_kernel(
                     h, gp = c // 4, c % 4
                     t = wpool.tile([P, 2, 1024], I32, tag="w", name="wo%d" % c, align_bytes=64)
                     cols = slice(1024 * h, 1024 * (h + 1))
-                    if c < 7:
+                    if c == 0:
+                        nc.sync.dma_start(out=t[:, 0, 0:512], in_=wo32[:, 0, 0:512])
+                        nc.sync.dma_start(out=t[:, 0, 512:1024], in_=wo32[:, 0, 512:1024])
+                        nc.sync.dma_start(out=t[:, 1, :], in_=wo32[:, 1, cols])
+                    elif c < 7:
                         nc.sync.dma_start(out=t[:], in_=wo32[:, 2 * gp : 2 * gp + 2, cols])
+                        if c == 1:
+                            load_out_scales(1)
                     else:
                         nc.sync.dma_start(out=t[:, 0, :], in_=wo32[:, 6, cols])
                         nc.sync.dma_start(out=t[:, 1, 0:512], in_=wo32[:, 7, 1024:1536])

@@ -40,6 +40,7 @@ def tile_jointnetwork_w_kernel(
         wpool = ctx.enter_context(tc.tile_pool(name="wpool", bufs=16))
         work = ctx.enter_context(tc.tile_pool(name="work", bufs=2))
         psum = ctx.enter_context(tc.psum_pool(name="psum", bufs=1))
+        ctx.enter_context(tc.manual_schedule())
 
         def bank(k, shape, name):
             return psum.tile(shape, F32, tag="b%d" % k, name=name)
@@ -155,85 +156,127 @@ def tile_jointnetwork_w_kernel(
         jp = const.tile([P, 8, 256], U8, align_bytes=64)
         planes = (pl_enc, pl_pred)
         wout = []
+        sums = {}
+        sorted_tiles = {}
+        flipped = {}
+        e1s = {}
+        zs = {}
+        jgs = {}
 
-        def stage1_sums(qt, n):
-            sums = [bank(2 * n + jj, [P, 512], "s1_%d_%d_%d" % (n, qt, jj)) for jj in range(2)]
-            for g in range(4):
+        def passes(qt, n, gp):
+            if gp == 0:
+                sums[(qt, n)] = [bank(2 * n + jj, [P, 512], "s1_%d_%d_%d" % (n, qt, jj)) for jj in range(2)]
+            for g in (2 * gp, 2 * gp + 1):
                 for jj in range(2):
                     nc.tensor.matmul_mx(
-                        out=sums[jj][:],
+                        out=sums[(qt, n)][jj][:],
                         lhsT=xq[n][:, P * g : P * (g + 1)].bitcast(FP8X4),
                         lhsT_scale=xs[n][:, P * g : P * (g + 1)],
-                        rhs=s1w[qt][n][g // 2][:, g % 2, 512 * jj : 512 * (jj + 1)].bitcast(FP8X4),
+                        rhs=s1w[qt][n][gp][:, g % 2, 512 * jj : 512 * (jj + 1)].bitcast(FP8X4),
                         rhs_scale=planes[n][4 * g : P, 1024 * qt + 512 * jj : 1024 * qt + 512 * (jj + 1)],
                         start=(g == 0),
                         stop=(g == 3),
                     )
-            sorted_tiles = []
+
+        def sort_out(qt, n):
+            tiles = []
             for jj in range(2):
                 srt = work.tile([P, 4, P], F32, tag="srt%d" % n, name="srt%d_%d_%d" % (n, qt, jj))
-                nc.scalar.copy(out=srt[:], in_=sums[jj][:].rearrange("r (p t) -> r t p", t=4))
-                sorted_tiles.append(srt)
-            flipped = []
+                nc.scalar.copy(out=srt[:], in_=sums[(qt, n)][jj][:].rearrange("r (p t) -> r t p", t=4))
+                tiles.append(srt)
+            sorted_tiles[(qt, n)] = tiles
+
+        def flip(qt, n):
+            tiles = []
             for jj in range(2):
                 fl = bank(4 + 2 * n + jj, [P, 4, P], "fl%d_%d_%d" % (n, qt, jj))
                 for t4 in range(4):
-                    nc.tensor.transpose(fl[:, t4, :], sorted_tiles[jj][:, t4, :], ident[:])
-                flipped.append(fl)
-            return flipped
+                    nc.tensor.transpose(fl[:, t4, :], sorted_tiles[(qt, n)][jj][:, t4, :], ident[:])
+                tiles.append(fl)
+            flipped[(qt, n)] = tiles
 
-        for qt in range(4):
-            enc_t = stage1_sums(qt, 0)
-            e1s = []
+        def add_bias(qt):
+            tiles = []
             for jj in range(2):
                 e1 = work.tile([P, P, 4], F32, tag="e1", name="e1_%d_%d" % (qt, jj))
                 nc.vector.tensor_tensor(
                     out=e1[:],
-                    in0=enc_t[jj][:].rearrange("p t r -> p r t"),
+                    in0=flipped[(qt, 0)][jj][:].rearrange("p t r -> p r t"),
                     in1=bias_j[:, 2 * qt + jj, :].unsqueeze(1).to_broadcast([P, P, 4]),
                     op=ADD,
                 )
-                e1s.append(e1)
-            pred_t = stage1_sums(qt, 1)
+                tiles.append(e1)
+            e1s[qt] = tiles
+
+        def add_pairs(qt, jj):
+            z = work.tile([P, 64, 2, 2, 4], F32, tag="z", name="z_%d_%d" % (qt, jj))
+            e1v = e1s[qt][jj][:].rearrange("p (b s) t -> p b s t", s=2)
+            pv = flipped[(qt, 1)][jj][:].rearrange("p t (b u) -> p b u t", u=2)
+            for s in range(2):
+                nc.vector.tensor_tensor(
+                    out=z[:, :, s, :, :],
+                    in0=pv,
+                    in1=e1v[:, :, s, :].unsqueeze(2).to_broadcast([P, 64, 2, 4]),
+                    op=ADD,
+                )
+            zs[(qt, jj)] = z
+
+        def squash(qt, jj):
+            jg = work.tile([P, 1024], BF16, tag="jg", name="jg_%d_%d" % (qt, jj), align_bytes=64)
+            nc.scalar.activation(out=jg[:], in_=zs[(qt, jj)][:].rearrange("p b s u t -> p (b s u t)"), func=TANH)
+            jgs[(qt, jj)] = jg
+
+        def quantise(qt, jj):
+            i = 2 * qt + jj
+            nc.vector.quantize_mx(out=jq[:, i, :].bitcast(FP8X4), scales=jp[:, i, :], in_=jgs[(qt, jj)][:])
+
+        def load_wout(c):
+            h, gp = c // 4, c % 4
+            t = wpool.tile([P, 2, 1024], I32, tag="w", name="wo%d" % c, align_bytes=64)
+            cols = slice(1024 * h, 1024 * (h + 1))
+            if c == 0:
+                nc.sync.dma_start(out=t[:, 0, 0:512], in_=wo32[:, 0, 0:512])
+                nc.sync.dma_start(out=t[:, 0, 512:1024], in_=wo32[:, 0, 512:1024])
+                nc.sync.dma_start(out=t[:, 1, :], in_=wo32[:, 1, cols])
+            elif c < 7:
+                nc.sync.dma_start(out=t[:], in_=wo32[:, 2 * gp : 2 * gp + 2, cols])
+                if c == 1:
+                    load_out_scales(1)
+            else:
+                nc.sync.dma_start(out=t[:, 0, :], in_=wo32[:, 6, cols])
+                nc.sync.dma_start(out=t[:, 1, 0:512], in_=wo32[:, 7, 1024:1536])
+                nc.sync.dma_start(out=t[:, 1, 512:1024], in_=wo32[:, 7, 1536:2048])
+            wout.append(t)
+
+        for qt in range(4):
+            passes(qt, 0, 0)
+            if qt > 0:
+                flip(qt - 1, 1)
+                add_pairs(qt - 1, 0)
+                add_pairs(qt - 1, 1)
+            passes(qt, 0, 1)
+            sort_out(qt, 0)
+            if qt > 0:
+                squash(qt - 1, 0)
+                squash(qt - 1, 1)
+            passes(qt, 1, 0)
+            flip(qt, 0)
+            add_bias(qt)
+            if qt > 0:
+                quantise(qt - 1, 0)
+                quantise(qt - 1, 1)
+            passes(qt, 1, 1)
+            sort_out(qt, 1)
             if qt < 2:
                 for c in range(4 * qt, 4 * qt + 4):
-                    h, gp = c // 4, c % 4
-                    t = wpool.tile([P, 2, 1024], I32, tag="w", name="wo%d" % c, align_bytes=64)
-                    cols = slice(1024 * h, 1024 * (h + 1))
-                    if c == 0:
-                        nc.sync.dma_start(out=t[:, 0, 0:512], in_=wo32[:, 0, 0:512])
-                        nc.sync.dma_start(out=t[:, 0, 512:1024], in_=wo32[:, 0, 512:1024])
-                        nc.sync.dma_start(out=t[:, 1, :], in_=wo32[:, 1, cols])
-                    elif c < 7:
-                        nc.sync.dma_start(out=t[:], in_=wo32[:, 2 * gp : 2 * gp + 2, cols])
-                        if c == 1:
-                            load_out_scales(1)
-                    else:
-                        nc.sync.dma_start(out=t[:, 0, :], in_=wo32[:, 6, cols])
-                        nc.sync.dma_start(out=t[:, 1, 0:512], in_=wo32[:, 7, 1024:1536])
-                        nc.sync.dma_start(out=t[:, 1, 512:1024], in_=wo32[:, 7, 1536:2048])
-                    wout.append(t)
-            zs = []
-            for jj in range(2):
-                z = work.tile([P, 64, 2, 2, 4], F32, tag="z", name="z_%d_%d" % (qt, jj))
-                e1v = e1s[jj][:].rearrange("p (b s) t -> p b s t", s=2)
-                pv = pred_t[jj][:].rearrange("p t (b u) -> p b u t", u=2)
-                for s in range(2):
-                    nc.vector.tensor_tensor(
-                        out=z[:, :, s, :, :],
-                        in0=pv,
-                        in1=e1v[:, :, s, :].unsqueeze(2).to_broadcast([P, 64, 2, 4]),
-                        op=ADD,
-                    )
-                zs.append(z)
-            jgs = []
-            for jj in range(2):
-                jg = work.tile([P, 1024], BF16, tag="jg", name="jg_%d_%d" % (qt, jj), align_bytes=64)
-                nc.scalar.activation(out=jg[:], in_=zs[jj][:].rearrange("p b s u t -> p (b s u t)"), func=TANH)
-                jgs.append(jg)
-            for jj in range(2):
-                i = 2 * qt + jj
-                nc.vector.quantize_mx(out=jq[:, i, :].bitcast(FP8X4), scales=jp[:, i, :], in_=jgs[jj][:])
+                    load_wout(c)
+        flip(3, 1)
+        for jj in range(2):
+            add_pairs(3, jj)
+        for jj in range(2):
+            squash(3, jj)
+        for jj in range(2):
+            quantise(3, jj)
 
         outf = out.flatten_outer_dims()
         for h in range(2):

@@ -279,22 +279,26 @@ def tile_jointnetwork_w_kernel(
             quantise(3, jj)
 
         outf = out.flatten_outer_dims()
+        LAST = 3
+
+        def out_pass(acc, h, g, nt, rt):
+            nc.tensor.matmul_mx(
+                out=acc[nt][rt][:],
+                lhsT=jq[:, g, P * rt : P * (rt + 1)].bitcast(FP8X4),
+                lhsT_scale=jp[:, g, P * rt : P * (rt + 1)],
+                rhs=wout[4 * h + g // 2][:, g % 2, 512 * nt : 512 * (nt + 1)].bitcast(FP8X4),
+                rhs_scale=pl_out[4 * (g % 4) : P, g // 4, 1024 * h + 512 * nt : 1024 * h + 512 * (nt + 1)],
+                start=(g == 0),
+                stop=(g == 7),
+            )
+
         for h in range(2):
             acc = [[bank(4 * h + 2 * nt + rt, [P, 512], "acc%d%d%d" % (h, nt, rt)) for rt in range(2)] for nt in range(2)]
-            for g in range(8):
-                wt = wout[4 * h + g // 2]
-                for nt in range(2):
-                    for rt in range(2):
-                        nc.tensor.matmul_mx(
-                            out=acc[nt][rt][:],
-                            lhsT=jq[:, g, P * rt : P * (rt + 1)].bitcast(FP8X4),
-                            lhsT_scale=jp[:, g, P * rt : P * (rt + 1)],
-                            rhs=wt[:, g % 2, 512 * nt : 512 * (nt + 1)].bitcast(FP8X4),
-                            rhs_scale=pl_out[4 * (g % 4) : P, g // 4, 1024 * h + 512 * nt : 1024 * h + 512 * (nt + 1)],
-                            start=(g == 0),
-                            stop=(g == 7),
-                        )
             if h == 0:
+                for g in range(8):
+                    for nt in range(2):
+                        for rt in range(2):
+                            out_pass(acc, h, g, nt, rt)
                 for rt in range(2):
                     st = work.tile([P, 1024], F32, tag="st", name="st%d" % rt)
                     for nt in range(2):
@@ -307,8 +311,14 @@ def tile_jointnetwork_w_kernel(
                     nc.gpsimd.tensor_scalar(out=st[:], in0=st[:], scalar1=CLAMP, scalar2=-CLAMP, op0=MIN, op1=MAX)
                     nc.sync.dma_start(out=outf[P * rt : P * (rt + 1), 0:1024], in_=st[:])
             else:
+                for g in range(8 - LAST):
+                    for nt in range(2):
+                        for rt in range(2):
+                            out_pass(acc, h, g, nt, rt)
                 for nt in range(2):
                     for rt in range(2):
+                        for g in range(8 - LAST, 8):
+                            out_pass(acc, h, g, nt, rt)
                         cols = slice(1024 + 512 * nt, 1024 + 512 * (nt + 1))
                         sl = work.tile([P, 512], F32, tag="sl", name="sl%d%d" % (nt, rt), bufs=4)
                         nc.vector.tensor_tensor(out=sl[:], in0=acc[nt][rt][:], in1=bias_out[:, cols], op=ADD)

@@ -83,15 +83,15 @@ def tile_jointnetwork_w_kernel(
         wo32 = W_out_words.bitcast(I32).rearrange("g p n o -> p g (n o)")
 
         s1w = []
-        for qt in range(4):
+        for hf in range(2):
             both = []
             for nm, w32 in (("e", we32), ("p", wp32)):
-                halves = []
-                for gp in range(2):
-                    t = wpool.tile([P, 2, 1024], I32, tag="w", name="w%s%d%d" % (nm, qt, gp), align_bytes=64)
-                    nc.sync.dma_start(out=t[:], in_=w32[:, 2 * gp : 2 * gp + 2, 1024 * qt : 1024 * (qt + 1)])
-                    halves.append(t)
-                both.append(halves)
+                groups = []
+                for g in range(4):
+                    t = wpool.tile([P, 2048], I32, tag="w", name="w%s%d%d" % (nm, hf, g), align_bytes=64)
+                    nc.sync.dma_start(out=t[:], in_=w32[:, g, 2048 * hf : 2048 * (hf + 1)])
+                    groups.append(t)
+                both.append(groups)
             s1w.append(both)
 
         so32 = W_out_scales.bitcast(I32)
@@ -163,55 +163,45 @@ def tile_jointnetwork_w_kernel(
         zs = {}
         jgs = {}
 
-        def passes(qt, n, gp):
-            if gp == 0:
-                sums[(qt, n)] = [bank(2 * n + jj, [P, 512], "s1_%d_%d_%d" % (n, qt, jj)) for jj in range(2)]
-            for g in (2 * gp, 2 * gp + 1):
-                for jj in range(2):
-                    nc.tensor.matmul_mx(
-                        out=sums[(qt, n)][jj][:],
-                        lhsT=xq[n][:, P * g : P * (g + 1)].bitcast(FP8X4),
-                        lhsT_scale=xs[n][:, P * g : P * (g + 1)],
-                        rhs=s1w[qt][n][gp][:, g % 2, 512 * jj : 512 * (jj + 1)].bitcast(FP8X4),
-                        rhs_scale=planes[n][4 * g : P, 1024 * qt + 512 * jj : 1024 * qt + 512 * (jj + 1)],
-                        start=(g == 0),
-                        stop=(g == 3),
-                    )
-
-        def sort_out(qt, n):
-            tiles = []
-            for jj in range(2):
-                srt = work.tile([P, 4, P], F32, tag="srt%d" % n, name="srt%d_%d_%d" % (n, qt, jj))
-                nc.scalar.copy(out=srt[:], in_=sums[(qt, n)][jj][:].rearrange("r (p t) -> r t p", t=4))
-                tiles.append(srt)
-            sorted_tiles[(qt, n)] = tiles
-
-        def flip(qt, n):
-            tiles = []
-            for jj in range(2):
-                fl = bank(4 + 2 * n + jj, [P, 4, P], "fl%d_%d_%d" % (n, qt, jj))
-                for t4 in range(4):
-                    nc.tensor.transpose(fl[:, t4, :], sorted_tiles[(qt, n)][jj][:, t4, :], ident[:])
-                tiles.append(fl)
-            flipped[(qt, n)] = tiles
-
-        def add_bias(qt):
-            tiles = []
-            for jj in range(2):
-                e1 = work.tile([P, P, 4], F32, tag="e1", name="e1_%d_%d" % (qt, jj))
-                nc.vector.tensor_tensor(
-                    out=e1[:],
-                    in0=flipped[(qt, 0)][jj][:].rearrange("p t r -> p r t"),
-                    in1=bias_j[:, 2 * qt + jj, :].unsqueeze(1).to_broadcast([P, P, 4]),
-                    op=ADD,
+        def passes(hf, n, g):
+            for jj in range(4):
+                if g == 0:
+                    sums[(hf, n, jj)] = bank(jj, [P, 512], "s1_%d_%d_%d" % (n, hf, jj))
+                nc.tensor.matmul_mx(
+                    out=sums[(hf, n, jj)][:],
+                    lhsT=xq[n][:, P * g : P * (g + 1)].bitcast(FP8X4),
+                    lhsT_scale=xs[n][:, P * g : P * (g + 1)],
+                    rhs=s1w[hf][n][g][:, 512 * jj : 512 * (jj + 1)].bitcast(FP8X4),
+                    rhs_scale=planes[n][4 * g : P, 2048 * hf + 512 * jj : 2048 * hf + 512 * (jj + 1)],
+                    start=(g == 0),
+                    stop=(g == 3),
                 )
-                tiles.append(e1)
-            e1s[qt] = tiles
 
-        def add_pairs(qt, jj):
-            z = work.tile([P, 64, 2, 2, 4], F32, tag="z", name="z_%d_%d" % (qt, jj))
-            e1v = e1s[qt][jj][:].rearrange("p (b s) t -> p b s t", s=2)
-            pv = flipped[(qt, 1)][jj][:].rearrange("p t (b u) -> p b u t", u=2)
+        def sort_out(hf, n, jj):
+            srt = work.tile([P, 4, P], F32, tag="srt", name="srt%d_%d_%d" % (n, hf, jj), bufs=4)
+            nc.scalar.copy(out=srt[:], in_=sums[(hf, n, jj)][:].rearrange("r (p t) -> r t p", t=4))
+            sorted_tiles[(hf, n, jj)] = srt
+
+        def flip(hf, n, jj):
+            fl = bank(4 + jj, [P, 4, P], "fl%d_%d_%d" % (n, hf, jj))
+            for t4 in range(4):
+                nc.tensor.transpose(fl[:, t4, :], sorted_tiles[(hf, n, jj)][:, t4, :], ident[:])
+            flipped[(hf, n, jj)] = fl
+
+        def add_bias(hf, jj):
+            e1 = work.tile([P, P, 4], F32, tag="e1", name="e1_%d_%d" % (hf, jj), bufs=4)
+            nc.vector.tensor_tensor(
+                out=e1[:],
+                in0=flipped[(hf, 0, jj)][:].rearrange("p t r -> p r t"),
+                in1=bias_j[:, 4 * hf + jj, :].unsqueeze(1).to_broadcast([P, P, 4]),
+                op=ADD,
+            )
+            e1s[(hf, jj)] = e1
+
+        def add_pairs(hf, jj):
+            z = work.tile([P, 64, 2, 2, 4], F32, tag="z", name="z_%d_%d" % (hf, jj), bufs=3)
+            e1v = e1s[(hf, jj)][:].rearrange("p (b s) t -> p b s t", s=2)
+            pv = flipped[(hf, 1, jj)][:].rearrange("p t (b u) -> p b u t", u=2)
             for s in range(2):
                 nc.vector.tensor_tensor(
                     out=z[:, :, s, :, :],
@@ -219,16 +209,16 @@ def tile_jointnetwork_w_kernel(
                     in1=e1v[:, :, s, :].unsqueeze(2).to_broadcast([P, 64, 2, 4]),
                     op=ADD,
                 )
-            zs[(qt, jj)] = z
+            zs[(hf, jj)] = z
 
-        def squash(qt, jj):
-            jg = work.tile([P, 1024], BF16, tag="jg", name="jg_%d_%d" % (qt, jj), align_bytes=64)
-            nc.scalar.activation(out=jg[:], in_=zs[(qt, jj)][:].rearrange("p b s u t -> p (b s u t)"), func=TANH)
-            jgs[(qt, jj)] = jg
+        def squash(hf, jj):
+            jg = work.tile([P, 1024], BF16, tag="jg", name="jg_%d_%d" % (hf, jj), align_bytes=64, bufs=4)
+            nc.scalar.activation(out=jg[:], in_=zs[(hf, jj)][:].rearrange("p b s u t -> p (b s u t)"), func=TANH)
+            jgs[(hf, jj)] = jg
 
-        def quantise(qt, jj):
-            i = 2 * qt + jj
-            nc.vector.quantize_mx(out=jq[:, i, :].bitcast(FP8X4), scales=jp[:, i, :], in_=jgs[(qt, jj)][:])
+        def quantise(hf, jj):
+            i = 4 * hf + jj
+            nc.vector.quantize_mx(out=jq[:, i, :].bitcast(FP8X4), scales=jp[:, i, :], in_=jgs[(hf, jj)][:])
 
         def load_wout(c):
             h, gp = c // 4, c % 4
@@ -248,35 +238,50 @@ def tile_jointnetwork_w_kernel(
                 nc.sync.dma_start(out=t[:, 1, 512:1024], in_=wo32[:, 7, 1536:2048])
             wout.append(t)
 
-        for qt in range(4):
-            passes(qt, 0, 0)
-            if qt > 0:
-                flip(qt - 1, 1)
-                add_pairs(qt - 1, 0)
-                add_pairs(qt - 1, 1)
-            passes(qt, 0, 1)
-            sort_out(qt, 0)
-            if qt > 0:
-                squash(qt - 1, 0)
-                squash(qt - 1, 1)
-            passes(qt, 1, 0)
-            flip(qt, 0)
-            add_bias(qt)
-            if qt > 0:
-                quantise(qt - 1, 0)
-                quantise(qt - 1, 1)
-            passes(qt, 1, 1)
-            sort_out(qt, 1)
-            if qt < 2:
-                for c in range(4 * qt, 4 * qt + 4):
+        def finish_first(hf):
+            for jj in range(4):
+                sort_out(hf, 1, jj)
+            for jj in range(2):
+                flip(hf, 1, jj)
+            for jj in range(2):
+                add_pairs(hf, jj)
+            squash(hf, 0)
+
+        def finish_rest(hf):
+            for jj in (2, 3):
+                flip(hf, 1, jj)
+            add_pairs(hf, 2)
+            quantise(hf, 0)
+            add_pairs(hf, 3)
+            for jj in (1, 2, 3):
+                squash(hf, jj)
+                quantise(hf, jj)
+
+        for hf in range(2):
+            passes(hf, 0, 0)
+            if hf > 0:
+                finish_rest(hf - 1)
+            for g in (1, 2, 3):
+                passes(hf, 0, g)
+            for jj in range(4):
+                sort_out(hf, 0, jj)
+            passes(hf, 1, 0)
+            for jj in (0, 1):
+                flip(hf, 0, jj)
+            for jj in (0, 1):
+                add_bias(hf, jj)
+            passes(hf, 1, 1)
+            for jj in (2, 3):
+                flip(hf, 0, jj)
+            for jj in (2, 3):
+                add_bias(hf, jj)
+            passes(hf, 1, 2)
+            passes(hf, 1, 3)
+            finish_first(hf)
+            if hf == 0:
+                for c in range(8):
                     load_wout(c)
-        flip(3, 1)
-        for jj in range(2):
-            add_pairs(3, jj)
-        for jj in range(2):
-            squash(3, jj)
-        for jj in range(2):
-            quantise(3, jj)
+        finish_rest(1)
 
         outf = out.flatten_outer_dims()
         LAST = 3
@@ -300,7 +305,7 @@ def tile_jointnetwork_w_kernel(
                         for rt in range(2):
                             out_pass(acc, h, g, nt, rt)
                 for rt in range(2):
-                    st = work.tile([P, 1024], F32, tag="st", name="st%d" % rt)
+                    st = work.tile([P, 1024], F32, tag="z", name="st%d" % rt, bufs=3)
                     for nt in range(2):
                         nc.vector.tensor_tensor(
                             out=st[:, 512 * nt : 512 * (nt + 1)],

@@ -229,7 +229,8 @@ def tile_jointnetwork_w_kernel(
                 nc.sync.dma_start(out=t[:, 0, 512:1024], in_=wo32[:, 0, 512:1024])
                 nc.sync.dma_start(out=t[:, 1, :], in_=wo32[:, 1, cols])
             elif c < 7:
-                nc.sync.dma_start(out=t[:], in_=wo32[:, 2 * gp : 2 * gp + 2, cols])
+                nc.sync.dma_start(out=t[:, 0, :], in_=wo32[:, 2 * gp, cols])
+                nc.sync.dma_start(out=t[:, 1, :], in_=wo32[:, 2 * gp + 1, cols])
                 if c == 1:
                     load_out_scales(1)
             else:

@@ -87,10 +87,19 @@ def tile_jointnetwork_w_kernel(
             both = []
             for nm, w32 in (("e", we32), ("p", wp32)):
                 groups = []
+                last = hf == 1 and nm == "p"
                 for g in range(4):
                     t = wpool.tile([P, 2048], I32, tag="w", name="w%s%d%d" % (nm, hf, g), align_bytes=64)
-                    nc.sync.dma_start(out=t[:], in_=w32[:, g, 2048 * hf : 2048 * (hf + 1)])
+                    if not (last and g >= 2):
+                        nc.sync.dma_start(out=t[:], in_=w32[:, g, 2048 * hf : 2048 * (hf + 1)])
                     groups.append(t)
+                if last:
+                    for c0 in (0, 1024):
+                        for g in (2, 3):
+                            nc.sync.dma_start(
+                                out=groups[g][:, c0 : c0 + 1024],
+                                in_=w32[:, g, 2048 + c0 : 2048 + c0 + 1024],
+                            )
                 both.append(groups)
             s1w.append(both)
 
@@ -163,8 +172,8 @@ def tile_jointnetwork_w_kernel(
         zs = {}
         jgs = {}
 
-        def passes(hf, n, g):
-            for jj in range(4):
+        def passes(hf, n, g, tiles=(0, 1, 2, 3)):
+            for jj in tiles:
                 if g == 0:
                     sums[(hf, n, jj)] = bank(jj, [P, 512], "s1_%d_%d_%d" % (n, hf, jj))
                 nc.tensor.matmul_mx(
@@ -177,9 +186,13 @@ def tile_jointnetwork_w_kernel(
                     stop=(g == 3),
                 )
 
-        def sort_out(hf, n, jj):
+        def sort_out(hf, n, jj, on_vector=False):
             srt = work.tile([P, 4, P], F32, tag="srt", name="srt%d_%d_%d" % (n, hf, jj), bufs=4)
-            nc.scalar.copy(out=srt[:], in_=sums[(hf, n, jj)][:].rearrange("r (p t) -> r t p", t=4))
+            src = sums[(hf, n, jj)][:].rearrange("r (p t) -> r t p", t=4)
+            if on_vector:
+                nc.vector.tensor_copy(out=srt[:], in_=src)
+            else:
+                nc.scalar.copy(out=srt[:], in_=src)
             sorted_tiles[(hf, n, jj)] = srt
 
         def flip(hf, n, jj):
@@ -276,13 +289,32 @@ def tile_jointnetwork_w_kernel(
                 flip(hf, 0, jj)
             for jj in (2, 3):
                 add_bias(hf, jj)
-            passes(hf, 1, 2)
-            passes(hf, 1, 3)
-            finish_first(hf)
             if hf == 0:
+                passes(hf, 1, 2)
+                passes(hf, 1, 3)
+                finish_first(hf)
                 for c in range(8):
                     load_wout(c)
-        finish_rest(1)
+        passes(1, 1, 2, (0, 1))
+        passes(1, 1, 3, (0, 1))
+        sort_out(1, 1, 0)
+        sort_out(1, 1, 1)
+        flip(1, 1, 0)
+        add_pairs(1, 0)
+        passes(1, 1, 2, (2, 3))
+        passes(1, 1, 3, (2, 3))
+        sort_out(1, 1, 2)
+        sort_out(1, 1, 3, on_vector=True)
+        squash(1, 0)
+        for jj in (1, 2, 3):
+            flip(1, 1, jj)
+        add_pairs(1, 1)
+        quantise(1, 0)
+        add_pairs(1, 2)
+        add_pairs(1, 3)
+        for jj in (1, 2, 3):
+            squash(1, jj)
+            quantise(1, jj)
 
         outf = out.flatten_outer_dims()
         LAST = 3

@@ -353,6 +353,13 @@ def tile_jointnetwork_w_kernel(
                     for nt in range(2):
                         for rt in range(2):
                             out_pass(acc, h, g, nt, rt)
+                waiting = []
+
+                def clamp_and_store():
+                    sl, rt, cols = waiting.pop(0)
+                    nc.vector.tensor_scalar(out=sl[:], in0=sl[:], scalar1=CLAMP, scalar2=-CLAMP, op0=MIN, op1=MAX)
+                    nc.sync.dma_start(out=outf[P * rt : P * (rt + 1), cols], in_=sl[:])
+
                 for nt in range(2):
                     for rt in range(2):
                         for g in range(8 - LAST, 8):
@@ -360,6 +367,7 @@ def tile_jointnetwork_w_kernel(
                         cols = slice(1024 + 512 * nt, 1024 + 512 * (nt + 1))
                         sl = work.tile([P, 512], F32, tag="sl", name="sl%d%d" % (nt, rt), bufs=4)
                         nc.vector.tensor_tensor(out=sl[:], in0=acc[nt][rt][:], in1=bias_out[:, cols], op=ADD)
-                        eng = nc.vector if (nt == 1 and rt == 1) else nc.gpsimd
-                        eng.tensor_scalar(out=sl[:], in0=sl[:], scalar1=CLAMP, scalar2=-CLAMP, op0=MIN, op1=MAX)
-                        nc.sync.dma_start(out=outf[P * rt : P * (rt + 1), cols], in_=sl[:])
+                        waiting.append((sl, rt, cols))
+                        if len(waiting) == 2:
+                            clamp_and_store()
+                clamp_and_store()

@@ -72,11 +72,12 @@ def tile_jointnetwork_w_kernel(
         nc.scalar.dma_start(out=brow[8:16, :], in_=b_pred.rearrange("(g c) -> g c", g=8))
         nc.scalar.dma_start(out=borow[0:1, :], in_=b_out.rearrange("(o n) -> o n", o=1))
 
-        for sc, pl in ((W_enc_scales, pl_enc), (W_pred_scales, pl_pred)):
-            sc32 = sc.bitcast(I32)
-            pl32 = pl[:].bitcast(I32)
-            for q in (0, 2, 1, 3):
-                nc.sync.dma_start(out=pl32[32 * q : 32 * q + 16, :], in_=sc32[:, 4 * q : 4 * q + 4, :])
+        for quads in ((2, 3), (0, 1)):
+            for sc, pl in ((W_enc_scales, pl_enc), (W_pred_scales, pl_pred)):
+                sc32 = sc.bitcast(I32)
+                pl32 = pl[:].bitcast(I32)
+                for q in quads:
+                    nc.sync.dma_start(out=pl32[32 * q : 32 * q + 16, :], in_=sc32[:, 4 * q : 4 * q + 4, :])
 
         we32 = W_enc_words.bitcast(I32).rearrange("g p n o -> p g (n o)")
         wp32 = W_pred_words.bitcast(I32).rearrange("g p n o -> p g (n o)")

@@ -45,9 +45,9 @@ def tile_jointnetwork_w_kernel(
         def bank(k, shape, name):
             return psum.tile(shape, F32, tag="b%d" % k, name=name)
 
-        pl_enc = const.tile([P, 4096], U8, align_bytes=64)
-        pl_pred = const.tile([P, 4096], U8, align_bytes=64)
-        pl_out = const.tile([P, 2, 2048], U8, align_bytes=64)
+        pl_enc = const.tile([P, 4096], U8, align_bytes=256)
+        pl_pred = const.tile([P, 4096], U8, align_bytes=256)
+        pl_out = const.tile([P, 2, 2048], U8, align_bytes=256)
         nc.vector.memset(pl_enc[:].bitcast(I32), 0)
         nc.vector.memset(pl_pred[:].bitcast(I32), 0)
         nc.vector.memset(pl_out[:].bitcast(I32), 0)
@@ -90,7 +90,7 @@ def tile_jointnetwork_w_kernel(
                 groups = []
                 last = hf == 1 and nm == "p"
                 for g in range(4):
-                    t = wpool.tile([P, 2048], I32, tag="w", name="w%s%d%d" % (nm, hf, g), align_bytes=64)
+                    t = wpool.tile([P, 2048], I32, tag="w", name="w%s%d%d" % (nm, hf, g), align_bytes=256)
                     if not (last and g >= 2):
                         nc.sync.dma_start(out=t[:], in_=w32[:, g, 2048 * hf : 2048 * (hf + 1)])
                     groups.append(t)
@@ -133,8 +133,8 @@ def tile_jointnetwork_w_kernel(
                     nc.vector.tensor_copy(out=grp32[:, 2 * gp : 2 * gp + 2, :, :], in_=src)
                 else:
                     nc.scalar.copy(out=grp32[:, 2 * gp : 2 * gp + 2, :, :], in_=src)
-            q_t = const.tile([P, 512], U32, name="xq" + nm, align_bytes=64)
-            s_t = const.tile([P, 512], U8, name="xs" + nm, align_bytes=64)
+            q_t = const.tile([P, 512], U32, name="xq" + nm, align_bytes=256)
+            s_t = const.tile([P, 512], U8, name="xs" + nm, align_bytes=256)
             nc.vector.quantize_mx(
                 out=q_t[:].bitcast(FP8X4),
                 scales=s_t[:],
@@ -162,8 +162,8 @@ def tile_jointnetwork_w_kernel(
         bcv = bc[:].rearrange("p r u e -> p r (u e)")
         nc.vector.tensor_tensor(out=bias_j[:], in0=bcv[:, 0:8, :], in1=bcv[:, 8:16, :], op=ADD)
 
-        jq = const.tile([P, 8, 256], U32, align_bytes=64)
-        jp = const.tile([P, 8, 256], U8, align_bytes=64)
+        jq = const.tile([P, 8, 256], U32, align_bytes=256)
+        jp = const.tile([P, 8, 256], U8, align_bytes=256)
         planes = (pl_enc, pl_pred)
         wout = []
         sums = {}
@@ -236,7 +236,7 @@ def tile_jointnetwork_w_kernel(
 
         def load_wout(c):
             h, gp = c // 4, c % 4
-            t = wpool.tile([P, 2, 1024], I32, tag="w", name="wo%d" % c, align_bytes=64)
+            t = wpool.tile([P, 2, 1024], I32, tag="w", name="wo%d" % c, align_bytes=256)
             cols = slice(1024 * h, 1024 * (h + 1))
             if c == 0:
                 nc.sync.dma_start(out=t[:, 0, 0:512], in_=wo32[:, 0, 0:512])

from contextlib import ExitStack

import concourse.mybir as mybir
from concourse.masks import make_identity

F32 = mybir.dt.float32
BF16 = mybir.dt.bfloat16
I32 = mybir.dt.int32
U32 = mybir.dt.uint32
U8 = mybir.dt.uint8
FP8X4 = mybir.dt.float8_e4m3fn_x4
ADD = mybir.AluOpType.add
MIN = mybir.AluOpType.min
MAX = mybir.AluOpType.max
TANH = mybir.ActivationFunctionType.Tanh

P = 128
FLOPS = 2 * 128 * 2048 * 4096 * 2 + 2 * 256 * 4096 * 2048
CLAMP = 15.0


def tile_jointnetwork_w_kernel(
    tc,
    encoder_out,
    predictor_out,
    W_enc_words,
    W_enc_scales,
    b_enc,
    W_pred_words,
    W_pred_scales,
    b_pred,
    W_out_words,
    W_out_scales,
    b_out,
    out,
):
    nc = tc.nc
    with ExitStack() as ctx:
        const = ctx.enter_context(tc.tile_pool(name="const", bufs=1))
        wpool = ctx.enter_context(tc.tile_pool(name="wpool", bufs=16))
        work = ctx.enter_context(tc.tile_pool(name="work", bufs=2))
        psum = ctx.enter_context(tc.psum_pool(name="psum", bufs=1))
        ctx.enter_context(tc.manual_schedule())

        def bank(k, shape, name):
            return psum.tile(shape, F32, tag="b%d" % k, name=name)

        pl_enc = const.tile([P, 4096], U8, align_bytes=256)
        pl_pred = const.tile([P, 4096], U8, align_bytes=256)
        pl_out = const.tile([P, 2, 2048], U8, align_bytes=256)
        nc.vector.memset(pl_enc[:].bitcast(I32), 0)
        nc.vector.memset(pl_pred[:].bitcast(I32), 0)
        nc.vector.memset(pl_out[:].bitcast(I32), 0)
        warm = const.tile([P, 1], F32)
        nc.vector.memset(warm[:], 0.0)
        nc.scalar.activation(out=warm[:], in_=warm[:], func=TANH)

        ident = const.tile([P, P], F32)
        make_identity(nc, ident[:])
        brow = const.tile([P, 512], BF16)
        nc.gpsimd.memset(brow[:].bitcast(F32), 0.0)
        borow = const.tile([P, 2048], BF16)
        nc.gpsimd.memset(borow[:].bitcast(F32), 0.0)
        ones = const.tile([P, P], BF16)
        nc.gpsimd.memset(ones[:], 1.0)

        xe = const.tile([P, 2048], BF16)
        xp = const.tile([P, 2048], BF16)
        nc.sync.dma_start(out=xe[:], in_=encoder_out.flatten_outer_dims())
        nc.sync.dma_start(out=xp[:], in_=predictor_out.flatten_outer_dims())
        nc.scalar.dma_start(out=brow[0:8, :], in_=b_enc.rearrange("(g c) -> g c", g=8))
        nc.scalar.dma_start(out=brow[8:16, :], in_=b_pred.rearrange("(g c) -> g c", g=8))
        nc.scalar.dma_start(out=borow[0:1, :], in_=b_out.rearrange("(o n) -> o n", o=1))

        for quads in ((2, 3), (0, 1)):
            for sc, pl in ((W_enc_scales, pl_enc), (W_pred_scales, pl_pred)):
                sc32 = sc.bitcast(I32)
                pl32 = pl[:].bitcast(I32)
                for q in quads:
                    nc.sync.dma_start(out=pl32[32 * q : 32 * q + 16, :], in_=sc32[:, 4 * q : 4 * q + 4, :])

        we32 = W_enc_words.bitcast(I32).rearrange("g p n o -> p g (n o)")
        wp32 = W_pred_words.bitcast(I32).rearrange("g p n o -> p g (n o)")
        wo32 = W_out_words.bitcast(I32).rearrange("g p n o -> p g (n o)")

        s1w = []
        for hf in range(2):
            both = []
            for nm, w32 in (("e", we32), ("p", wp32)):
                groups = []
                last = hf == 1 and nm == "p"
                for g in range(4):
                    t = wpool.tile([P, 2048], I32, tag="w", name="w%s%d%d" % (nm, hf, g), align_bytes=256)
                    if not (last and g >= 2):
                        nc.sync.dma_start(out=t[:], in_=w32[:, g, 2048 * hf : 2048 * (hf + 1)])
                    groups.append(t)
                if last:
                    for c0 in (0, 1024):
                        for g in (2, 3):
                            nc.sync.dma_start(
                                out=groups[g][:, c0 : c0 + 1024],
                                in_=w32[:, g, 2048 + c0 : 2048 + c0 + 1024],
                            )
                both.append(groups)
            s1w.append(both)

        so32 = W_out_scales.bitcast(I32)
        po32 = pl_out[:].bitcast(I32)

        def load_out_scales(a):
            for q in (0, 2, 1, 3):
                nc.sync.dma_start(
                    out=po32[32 * q : 32 * q + 16, a, :],
                    in_=so32[4 * a : 4 * a + 4, 4 * q : 4 * q + 4, :],
                )

        load_out_scales(0)

        xq = []
        xs = []
        for n, (x_sb, nm) in enumerate(((xe, "e"), (xp, "p"))):
            xw = x_sb[:].bitcast(F32)
            grp = const.tile([P, 4, P, 4], BF16, name="grp" + nm, align_bytes=64)
            grp32 = grp[:].rearrange("p g r t -> p g (r t)").bitcast(F32).rearrange("p g (r u) -> p g r u", u=2)
            for gp in range(2):
                xt = bank(2 * n + gp, [P, 2, 2, P], "xt%s%d" % (nm, gp))
                for gg in range(2):
                    g = 2 * gp + gg
                    for u in range(2):
                        nc.tensor.transpose(xt[:, gg, u, :], xw[:, 256 * g + u : 256 * (g + 1) : 2], ident[:])
                src = xt[:].rearrange("p g u r -> p g r u")
                if n == 0:
                    nc.vector.tensor_copy(out=grp32[:, 2 * gp : 2 * gp + 2, :, :], in_=src)
                else:
                    nc.scalar.copy(out=grp32[:, 2 * gp : 2 * gp + 2, :, :], in_=src)
            q_t = const.tile([P, 512], U32, name="xq" + nm, align_bytes=256)
            s_t = const.tile([P, 512], U8, name="xs" + nm, align_bytes=256)
            nc.vector.quantize_mx(
                out=q_t[:].bitcast(FP8X4),
                scales=s_t[:],
                in_=grp[:].rearrange("p g r t -> p (g r t)"),
            )
            xq.append(q_t)
            xs.append(s_t)

        bias_out = const.tile([P, 2048], F32)
        for c in range(4):
            bo = bank(4 + c, [P, 512], "bo%d" % c)
            nc.tensor.matmul(out=bo[:], lhsT=ones[:], rhs=borow[:, 512 * c : 512 * (c + 1)], start=True, stop=True)
            if c % 2 == 0:
                nc.vector.tensor_copy(out=bias_out[:, 512 * c : 512 * (c + 1)], in_=bo[:])
            else:
                nc.scalar.copy(out=bias_out[:, 512 * c : 512 * (c + 1)], in_=bo[:])
        bt = bank(4, [P, 2, P], "bt")
        bw = brow[:].bitcast(F32)
        for u in range(2):
            nc.tensor.transpose(bt[:, u, :], bw[:, u : 256 : 2], ident[:])
        bc = const.tile([P, 16, 2, 2], F32)
        btv = bt[:].bitcast(BF16).rearrange("p u (r e) -> p u r e", e=2)
        nc.vector.tensor_copy(out=bc[:], in_=btv[:, :, 0:16, :].rearrange("p u r e -> p r u e"))
        bias_j = const.tile([P, 8, 4], F32)
        bcv = bc[:].rearrange("p r u e -> p r (u e)")
        nc.vector.tensor_tensor(out=bias_j[:], in0=bcv[:, 0:8, :], in1=bcv[:, 8:16, :], op=ADD)

        jq = const.tile([P, 8, 256], U32, align_bytes=256)
        jp = const.tile([P, 8, 256], U8, align_bytes=256)
        planes = (pl_enc, pl_pred)
        wout = []
        sums = {}
        sorted_tiles = {}
        flipped = {}
        e1s = {}
        zs = {}
        jgs = {}

        def passes(hf, n, g, tiles=(0, 1, 2, 3)):
            for jj in tiles:
                if g == 0:
                    sums[(hf, n, jj)] = bank(jj, [P, 512], "s1_%d_%d_%d" % (n, hf, jj))
                nc.tensor.matmul_mx(
                    out=sums[(hf, n, jj)][:],
                    lhsT=xq[n][:, P * g : P * (g + 1)].bitcast(FP8X4),
                    lhsT_scale=xs[n][:, P * g : P * (g + 1)],
                    rhs=s1w[hf][n][g][:, 512 * jj : 512 * (jj + 1)].bitcast(FP8X4),
                    rhs_scale=planes[n][4 * g : P, 2048 * hf + 512 * jj : 2048 * hf + 512 * (jj + 1)],
                    start=(g == 0),
                    stop=(g == 3),
                )

        def sort_out(hf, n, jj, on_vector=False):
            srt = work.tile([P, 4, P], F32, tag="srt", name="srt%d_%d_%d" % (n, hf, jj), bufs=4)
            src = sums[(hf, n, jj)][:].rearrange("r (p t) -> r t p", t=4)
            if on_vector:
                nc.vector.tensor_copy(out=srt[:], in_=src)
            else:
                nc.scalar.copy(out=srt[:], in_=src)
            sorted_tiles[(hf, n, jj)] = srt

        def flip(hf, n, jj):
            fl = bank(4 + jj, [P, 4, P], "fl%d_%d_%d" % (n, hf, jj))
            for t4 in range(4):
                nc.tensor.transpose(fl[:, t4, :], sorted_tiles[(hf, n, jj)][:, t4, :], ident[:])
            flipped[(hf, n, jj)] = fl

        def add_bias(hf, jj):
            e1 = work.tile([P, P, 4], F32, tag="e1", name="e1_%d_%d" % (hf, jj), bufs=4)
            nc.vector.tensor_tensor(
                out=e1[:],
                in0=flipped[(hf, 0, jj)][:].rearrange("p t r -> p r t"),
                in1=bias_j[:, 4 * hf + jj, :].unsqueeze(1).to_broadcast([P, P, 4]),
                op=ADD,
            )
            e1s[(hf, jj)] = e1

        def add_pairs(hf, jj):
            z = work.tile([P, 64, 2, 2, 4], F32, tag="z", name="z_%d_%d" % (hf, jj), bufs=3)
            e1v = e1s[(hf, jj)][:].rearrange("p (b s) t -> p b s t", s=2)
            pv = flipped[(hf, 1, jj)][:].rearrange("p t (b u) -> p b u t", u=2)
            for s in range(2):
                nc.vector.tensor_tensor(
                    out=z[:, :, s, :, :],
                    in0=pv,
                    in1=e1v[:, :, s, :].unsqueeze(2).to_broadcast([P, 64, 2, 4]),
                    op=ADD,
                )
            zs[(hf, jj)] = z

        def squash(hf, jj):
            jg = work.tile([P, 1024], BF16, tag="jg", name="jg_%d_%d" % (hf, jj), align_bytes=64, bufs=4)
            nc.scalar.activation(out=jg[:], in_=zs[(hf, jj)][:].rearrange("p b s u t -> p (b s u t)"), func=TANH)
            jgs[(hf, jj)] = jg

        def quantise(hf, jj):
            i = 4 * hf + jj
            nc.vector.quantize_mx(out=jq[:, i, :].bitcast(FP8X4), scales=jp[:, i, :], in_=jgs[(hf, jj)][:])

        def load_wout(c):
            h, gp = c // 4, c % 4
            t = wpool.tile([P, 2, 1024], I32, tag="w", name="wo%d" % c, align_bytes=256)
            cols = slice(1024 * h, 1024 * (h + 1))
            if c == 0:
                nc.sync.dma_start(out=t[:, 0, 0:512], in_=wo32[:, 0, 0:512])
                nc.sync.dma_start(out=t[:, 0, 512:1024], in_=wo32[:, 0, 512:1024])
                nc.sync.dma_start(out=t[:, 1, :], in_=wo32[:, 1, cols])
            elif c < 7:
                nc.sync.dma_start(out=t[:, 0, :], in_=wo32[:, 2 * gp, cols])
                nc.sync.dma_start(out=t[:, 1, :], in_=wo32[:, 2 * gp + 1, cols])
                if c == 1:
                    load_out_scales(1)
            else:
                nc.sync.dma_start(out=t[:, 0, :], in_=wo32[:, 6, cols])
                nc.sync.dma_start(out=t[:, 1, 0:512], in_=wo32[:, 7, 1024:1536])
                nc.sync.dma_start(out=t[:, 1, 512:1024], in_=wo32[:, 7, 1536:2048])
            wout.append(t)

        def finish_first(hf):
            for jj in range(4):
                sort_out(hf, 1, jj)
            for jj in range(2):
                flip(hf, 1, jj)
            for jj in range(2):
                add_pairs(hf, jj)
            squash(hf, 0)

        def finish_rest(hf):
            for jj in (2, 3):
                flip(hf, 1, jj)
            add_pairs(hf, 2)
            quantise(hf, 0)
            add_pairs(hf, 3)
            for jj in (1, 2, 3):
                squash(hf, jj)
                quantise(hf, jj)

        for hf in range(2):
            passes(hf, 0, 0)
            if hf > 0:
                finish_rest(hf - 1)
            for g in (1, 2, 3):
                passes(hf, 0, g)
            for jj in range(4):
                sort_out(hf, 0, jj)
            passes(hf, 1, 0)
            for jj in (0, 1):
                flip(hf, 0, jj)
            for jj in (0, 1):
                add_bias(hf, jj)
            passes(hf, 1, 1)
            for jj in (2, 3):
                flip(hf, 0, jj)
            for jj in (2, 3):
                add_bias(hf, jj)
            if hf == 0:
                passes(hf, 1, 2)
                passes(hf, 1, 3)
                finish_first(hf)
                for c in range(8):
                    load_wout(c)
        passes(1, 1, 2, (0, 1))
        passes(1, 1, 3, (0, 1))
        sort_out(1, 1, 0)
        sort_out(1, 1, 1)
        flip(1, 1, 0)
        add_pairs(1, 0)
        passes(1, 1, 2, (2, 3))
        passes(1, 1, 3, (2, 3))
        sort_out(1, 1, 2)
        sort_out(1, 1, 3, on_vector=True)
        squash(1, 0)
        for jj in (1, 2, 3):
            flip(1, 1, jj)
        add_pairs(1, 1)
        quantise(1, 0)
        add_pairs(1, 2)
        add_pairs(1, 3)
        for jj in (1, 2, 3):
            squash(1, jj)
            quantise(1, jj)

        outf = out.flatten_outer_dims()
        LAST = 3

        def out_pass(acc, h, g, nt, rt):
            nc.tensor.matmul_mx(
                out=acc[nt][rt][:],
                lhsT=jq[:, g, P * rt : P * (rt + 1)].bitcast(FP8X4),
                lhsT_scale=jp[:, g, P * rt : P * (rt + 1)],
                rhs=wout[4 * h + g // 2][:, g % 2, 512 * nt : 512 * (nt + 1)].bitcast(FP8X4),
                rhs_scale=pl_out[4 * (g % 4) : P, g // 4, 1024 * h + 512 * nt : 1024 * h + 512 * (nt + 1)],
                start=(g == 0),
                stop=(g == 7),
            )

        for h in range(2):
            acc = [[bank(4 * h + 2 * nt + rt, [P, 512], "acc%d%d%d" % (h, nt, rt)) for rt in range(2)] for nt in range(2)]
            if h == 0:
                for g in range(8):
                    for nt in range(2):
                        for rt in range(2):
                            out_pass(acc, h, g, nt, rt)
                for rt in range(2):
                    st = work.tile([P, 1024], F32, tag="z", name="st%d" % rt, bufs=3)
                    for nt in range(2):
                        nc.vector.tensor_tensor(
                            out=st[:, 512 * nt : 512 * (nt + 1)],
                            in0=acc[nt][rt][:],
                            in1=bias_out[:, 512 * nt : 512 * (nt + 1)],
                            op=ADD,
                        )
                    nc.gpsimd.tensor_scalar(out=st[:], in0=st[:], scalar1=CLAMP, scalar2=-CLAMP, op0=MIN, op1=MAX)
                    nc.sync.dma_start(out=outf[P * rt : P * (rt + 1), 0:1024], in_=st[:])
            else:
                for g in range(8 - LAST):
                    for nt in range(2):
                        for rt in range(2):
                            out_pass(acc, h, g, nt, rt)
                waiting = []

                def clamp_and_store():
                    sl, rt, cols = waiting.pop(0)
                    nc.vector.tensor_scalar(out=sl[:], in0=sl[:], scalar1=CLAMP, scalar2=-CLAMP, op0=MIN, op1=MAX)
                    nc.sync.dma_start(out=outf[P * rt : P * (rt + 1), cols], in_=sl[:])

                for nt in range(2):
                    for rt in range(2):
                        for g in range(8 - LAST, 8):
                            out_pass(acc, h, g, nt, rt)
                        cols = slice(1024 + 512 * nt, 1024 + 512 * (nt + 1))
                        sl = work.tile([P, 512], F32, tag="sl", name="sl%d%d" % (nt, rt), bufs=4)
                        nc.vector.tensor_tensor(out=sl[:], in0=acc[nt][rt][:], in1=bias_out[:, cols], op=ADD)
                        waiting.append((sl, rt, cols))
                        if len(waiting) == 2:
                            clamp_and_store()
                clamp_and_store()
